import numpy as np
import ml_dtypes


def mxq(x, axis, fmt="e4m3"):
    dtype, down = {"e4m3": (ml_dtypes.float8_e4m3fn, 7), "e5m2": (ml_dtypes.float8_e5m2, 14)}[fmt]
    v = np.moveaxis(np.asarray(x, np.float32).astype(ml_dtypes.bfloat16).astype(np.float64), axis, -1)
    blocks = v.reshape(v.shape[:-1] + (-1, 32))
    amax = np.abs(blocks).max(-1, keepdims=True)
    byte = np.maximum(np.where(amax > 0, np.frexp(amax)[1] - 1 + 127, 0) - down, 1)
    scale = np.exp2(byte - 127.0)
    codes = (blocks / scale).astype(np.float32).astype(dtype).astype(np.float64)
    return np.moveaxis((codes * scale).reshape(v.shape), -1, axis)


WIDE = False


def mx_kscale(k):
    if not WIDE:
        return np.ones(k)
    levels = np.array([10, -10, 5, -5, 0])
    a = np.random.permutation(np.resize(levels, k // 512 * 4)).reshape(k // 512, 4)
    idx = np.arange(k)
    return np.exp2(a[idx // 512, idx % 128 // 32])


BF16 = ml_dtypes.bfloat16


def bf(x):
    return np.asarray(x, np.float32).astype(BF16)


def f64(x):
    return np.asarray(x).astype(np.float64)


N, D, B = 4096, 256, 3072


def setup_inputs():
    f = np.concatenate([np.ones(B), mx_kscale(N)[B:]])
    g = np.mean(f)
    return {"adjacency_matrix": bf(np.random.uniform(size=(N, N)) * f[None, :]),
            "node_features": bf(np.random.standard_normal((N, D)) / f[:, None]),
            "W_gcn": bf(np.random.standard_normal((D, D)) * 0.25 * np.sqrt(N) / np.sqrt(D) * g),
            "W_skip": bf(np.random.standard_normal((D, D)) * 0.5 / np.sqrt(D)),
            "batch_size": B}


def reference(adjacency_matrix, node_features, W_gcn, W_skip, batch_size):
    beta = 0.5
    a = f64(adjacency_matrix)
    x = f64(node_features)
    deg = np.sum(a, axis=1)
    d_inv_sqrt = 1.0 / np.sqrt(deg + 1e-8)
    normalized_adj = d_inv_sqrt[:, None] * a * d_inv_sqrt[None, :]
    h = x @ f64(W_gcn).T
    adj_rows = normalized_adj[:batch_size]
    gcn_out = np.maximum((mxq(adj_rows, 1, "e4m3") @ mxq(h, 0, "e4m3")) + x[:batch_size] @ f64(W_skip).T, 0.0)
    sample_features = gcn_out[:batch_size]
    original_features = x[:batch_size]
    enhanced_features = original_features + beta * sample_features
    return enhanced_features

@@ -1,0 +1,212 @@
+from contextlib import ExitStack
+
+import concourse.bass as bass
+import concourse.mybir as mybir
+import concourse.tile as tile
+from concourse.masks import make_identity
+
+F32 = mybir.dt.float32
+BF16 = mybir.dt.bfloat16
+U8 = mybir.dt.uint8
+U32 = mybir.dt.uint32
+FP8X4 = mybir.dt.float8_e4m3fn_x4
+ALU = mybir.AluOpType
+ACT = mybir.ActivationFunctionType
+
+P = 128
+NODES = 4096
+FEAT = 256
+ROWS = 3072
+NBLK = NODES // P
+MBLK = ROWS // P
+PASS = 512
+NPASS = NODES // PASS
+LOAD_ORDER = [0, 1, 2, 3, 4, 5, 6, 7]
+OPEN = [0, 1]
+A_SLOTS = 20
+NAT1 = "gsvgsvgs"
+NAT2 = "sgsg"
+
+FLOPS = 2 * ROWS * NODES * FEAT + 2 * NODES * FEAT * FEAT + 2 * ROWS * FEAT * FEAT
+
+
+def tile_structureawaregcn_t_kernel(tc, adjacency_matrix, node_features, W_gcn, W_skip, batch_size, out):
+    nc = tc.nc
+    x_blocks = node_features.rearrange("(b p) d -> p b d", p=P)
+    out_blocks = out.rearrange("(b p) c -> p b c", p=P)
+    with ExitStack() as ctx:
+        const = ctx.enter_context(tc.tile_pool(name="const", bufs=1))
+        apool = ctx.enter_context(tc.tile_pool(name="apool", bufs=A_SLOTS))
+        stage = ctx.enter_context(tc.tile_pool(name="stage", bufs=6))
+        gpool = ctx.enter_context(tc.tile_pool(name="gpool", bufs=2))
+        cpool = ctx.enter_context(tc.tile_pool(name="cpool", bufs=3))
+        epool = ctx.enter_context(tc.tile_pool(name="epool", bufs=2))
+        psum = ctx.enter_context(tc.psum_pool(name="psum", bufs=4))
+
+        ident_f = const.tile([P, P], F32, name="ident_f")
+        ident_b = const.tile([P, P], BF16, name="ident_b")
+        make_identity(nc, ident_f[:])
+        make_identity(nc, ident_b[:])
+        wT = const.tile([P, 2, 2, FEAT], BF16, name="wT")
+        hc = const.tile([P, NPASS, FEAT], U32, name="hc", align_bytes=64)
+        hs = const.tile([P, NPASS, FEAT], U8, name="hs", align_bytes=64)
+        xT = const.tile([P, 2, ROWS], BF16, name="xT")
+        deg = const.tile([P, NBLK, 8], F32, name="deg")
+        sq = const.tile([P, NBLK], F32, name="sq")
+        dinv = const.tile([P, NBLK], F32, name="dinv")
+        warm = const.tile([P, 1], F32, name="warm")
+        nc.vector.memset(warm[:], 1.0)
+        nc.scalar.activation(out=warm[:], in_=warm[:], func=ACT.Sqrt)
+
+        a_tiles = {}
+
+        def load_chunk(c):
+            for blk in range(4 * c, 4 * c + 4):
+                a_t = apool.tile([P, NODES], BF16, name="a_t", tag="a", align_bytes=64)
+                nc.sync.dma_start(out=a_t[:], in_=adjacency_matrix[P * blk : P * blk + P, :])
+                a_tiles[blk] = a_t
+
+        def degrees(c):
+            for blk in range(4 * c, 4 * c + 4):
+                a_t = a_tiles[blk]
+                if blk % 2 == 0:
+                    nc.vector.tensor_scalar(out=a_t[:], in0=a_t[:], scalar1=1.0, scalar2=None, op0=ALU.mult, op1=ALU.add, accum_out=deg[:, blk, 0:1])
+                else:
+                    nc.scalar.activation(out=a_t[:], in_=a_t[:], func=ACT.Copy, accum_out=deg[:, blk, 0:1])
+            cols = slice(4 * c, 4 * c + 4)
+            nc.scalar.activation(out=sq[:, cols], in_=deg[:, cols, 0], func=ACT.Sqrt, bias=1e-8)
+            nc.vector.reciprocal(out=dinv[:, cols], in_=sq[:, cols])
+
+        scratch = apool.tile([P, NODES], BF16, name="scratch", tag="a", align_bytes=64)
+        w_nat = scratch[:, 3072:4096].rearrange("p (w h d) -> p w h d", w=2, h=2)
+        xT_tail = scratch[:, 0:2048].rearrange("p (h n) -> p h n", h=2)
+        gh = scratch[:, 2048:3072].rearrange("p (c t) -> p c t", t=4)
+        nc.sync.dma_start(out=w_nat[:, 0], in_=W_gcn.rearrange("(h p) d -> p h d", p=P))
+        nc.sync.dma_start(out=w_nat[:, 1], in_=W_skip.rearrange("(h p) d -> p h d", p=P))
+        load_chunk(LOAD_ORDER[0])
+        x_nat = []
+        for half in range(2):
+            x_t = apool.tile([P, NODES], BF16, name="x_t", tag="a", align_bytes=64)
+            x_v = x_t[:].rearrange("p (b d) -> p b d", d=FEAT)
+            nc.sync.dma_start(out=x_v, in_=x_blocks[:, 16 * half : 16 * half + 16, :])
+            x_nat.append(x_v)
+        for c in LOAD_ORDER[1:]:
+            load_chunk(c)
+
+        def features():
+            wps = psum.tile([P, 2, 2, 2, P], BF16, name="wps", tag="T")
+            for w in range(2):
+                for dh in range(2):
+                    for oh in range(2):
+                        nc.tensor.transpose(wps[:, w, dh, oh, :], w_nat[:, w, oh, P * dh : P * dh + P], ident_b[:])
+            nc.scalar.copy(out=wT[:].rearrange("p w h o -> p (w h o)"), in_=wps[:].rearrange("p w h q o -> p (w h q o)"))
+            for q in range(4):
+                for dh in range(2):
+                    xps = psum.tile([P, 8, P], BF16, name="xps", tag="T")
+                    for nb in range(8):
+                        blk = 8 * q + nb
+                        nc.tensor.transpose(xps[:, nb, :], x_nat[blk // 16][:, blk % 16, P * dh : P * dh + P], ident_b[:])
+                    dst = xT[:, dh, 1024 * q : 1024 * q + 1024] if q < 3 else xT_tail[:, dh, :]
+                    nc.scalar.copy(out=dst, in_=xps[:].rearrange("p b n -> p (b n)"))
+            for g in range(NPASS):
+                for ch in range(2):
+                    hps = psum.tile([P, 4, P], F32, name="hps", tag="T")
+                    for t in range(4):
+                        blk = 4 * g + t
+                        for dh in range(2):
+                            lhsT = xT[:, dh, P * blk : P * blk + P] if blk < MBLK else xT_tail[:, dh, P * (blk - MBLK) : P * (blk - MBLK) + P]
+                            nc.tensor.matmul(out=hps[:, t, :], lhsT=lhsT, rhs=wT[:, 0, dh, P * ch : P * ch + P], start=(dh == 0), stop=(dh == 1))
+                    nc.scalar.copy(out=gh[:, P * ch : P * ch + P, :], in_=hps[:].rearrange("p t c -> p c t"))
+                nc.vector.quantize_mx(out=hc[:, g, :].bitcast(FP8X4), scales=hs[:, g, :], in_=gh.rearrange("p c t -> p (c t)"))
+
+        counter = [0]
+        pending = []
+        acc = {}
+        seen = {}
+
+        def flush_pending():
+            while pending:
+                m, g, grp = pending.pop(0)
+                codes = cpool.tile([P, PASS], U32, name="codes", align_bytes=64)
+                scl = cpool.tile([P, PASS], U8, name="scl", align_bytes=64)
+                nc.vector.quantize_mx(out=codes[:].bitcast(FP8X4), scales=scl[:], in_=grp[:].rearrange("p r t -> p (r t)"))
+                seen[m] = seen.get(m, 0) + 1
+                for ch in range(2):
+                    nc.tensor.matmul_mx(out=acc[m][ch][:], lhsT=hc[:, g, P * ch : P * ch + P].bitcast(FP8X4), lhsT_scale=hs[:, g, P * ch : P * ch + P], rhs=codes[:].bitcast(FP8X4), rhs_scale=scl[:], start=(seen[m] == 1), stop=(seen[m] == NPASS))
+
+        def pair(m, g, pattern):
+            if m not in acc:
+                acc[m] = [psum.tile([P, PASS], F32, name="acc", tag="acc") for ch in range(2)]
+            grp = gpool.tile([P, PASS, 4], BF16, name="grp", align_bytes=64)
+            for j in range(4):
+                b = 4 * m + j
+                src = a_tiles[b][:, PASS * g : PASS * g + PASS]
+                f = stage.tile([P, PASS], F32, name="f")
+                eng = pattern[counter[0] % len(pattern)]
+                counter[0] += 1
+                if eng == "g":
+                    nc.gpsimd.tensor_scalar(out=f[:], in0=src, scalar1=dinv[:, b : b + 1], scalar2=0.0, op0=ALU.mult, op1=ALU.add)
+                elif eng == "s":
+                    nc.scalar.activation(out=f[:], in_=src, func=ACT.Copy, scale=dinv[:, b : b + 1])
+                else:
+                    nc.vector.tensor_scalar(out=f[:], in0=src, scalar1=dinv[:, b : b + 1], scalar2=None, op0=ALU.mult)
+                bank = psum.tile([P, 4, P], F32, name="bank", tag="T")
+                for t in range(4):
+                    nc.tensor.transpose(bank[:, t, :], f[:, P * t : P * t + P], ident_f[:])
+                nc.vector.tensor_tensor(out=grp[:, P * j : P * j + P, :], in0=bank[:].rearrange("p t r -> p r t"), in1=dinv[:, 4 * g : 4 * g + 4].unsqueeze(1).to_broadcast([P, P, 4]), op=ALU.mult)
+                if j == 0:
+                    flush_pending()
+            pending.append((m, g, grp))
+
+        def skip_term(m):
+            ws = []
+            for ch in range(2):
+                skp = psum.tile([P, PASS], F32, name="skp", tag="T")
+                for dh in range(2):
+                    nc.tensor.matmul(out=skp[:], lhsT=wT[:, 1, dh, P * ch : P * ch + P], rhs=xT[:, dh, PASS * m : PASS * m + PASS], start=(dh == 0), stop=(dh == 1))
+                w = epool.tile([P, PASS], F32, name="w%d" % ch)
+                nc.scalar.activation(out=w[:], in_=skp[:], func=ACT.Copy, scale=0.5)
+                ws.append(w)
+            return ws
+
+        def finish(m, ws):
+            for ch in range(2):
+                w = ws[ch]
+                nc.vector.scalar_tensor_tensor(out=w[:], in0=acc[m][ch][:], scalar=0.5, in1=w[:], op0=ALU.mult, op1=ALU.add)
+                nc.vector.scalar_tensor_tensor(out=w[:], in0=w[:], scalar=0.0, in1=xT[:, ch, PASS * m : PASS * m + PASS], op0=ALU.max, op1=ALU.add)
+            for jp in range(2):
+                bo = psum.tile([P, 2, 2, P], F32, name="bo", tag="T")
+                for j in range(2):
+                    for ch in range(2):
+                        col = P * (2 * jp + j)
+                        nc.tensor.transpose(bo[:, j, ch, :], ws[ch][:, col : col + P], ident_f[:])
+                o = epool.tile([P, 2, FEAT], F32, name="o")
+                nc.scalar.copy(out=o[:].rearrange("p j c -> p (j c)"), in_=bo[:].rearrange("p j h c -> p (j h c)"))
+                nc.sync.dma_start(out=out_blocks[:, 4 * m + 2 * jp : 4 * m + 2 * jp + 2, :], in_=o[:])
+
+        known = []
+        ws_open = {}
+        for step, c in enumerate(LOAD_ORDER):
+            degrees(c)
+            if step == 0:
+                features()
+            known.append(c)
+            for m in OPEN:
+                if m == c:
+                    ws_open[m] = skip_term(m)
+                    for g in known:
+                        pair(m, g, NAT1)
+                elif m in known:
+                    pair(m, c, NAT1)
+        flush_pending()
+        for m in OPEN:
+            finish(m, ws_open[m])
+        for m in range(ROWS // PASS):
+            if m in OPEN:
+                continue
+            load_chunk(m)
+            ws = skip_term(m)
+            for g in range(NPASS):
+                pair(m, g, NAT2)
+            flush_pending()
+            finish(m, ws)

@@ -21,32 +21,65 @@ NBLK = NODES // P
 MBLK = ROWS // P
 PASS = 512
 NPASS = NODES // PASS
-LOAD_ORDER = [0, 1, 2, 3, 4, 5, 6, 7]
+NCHUNK = ROWS // PASS
 OPEN = [0, 1]
-A_SLOTS = 20
-NAT1 = "gsvgsvgs"
-NAT2 = "sgsg"
+A_SLOTS = 9
+LAG = 2
+FIN_DELAY = 2
+PREP_AT = 3
 
 FLOPS = 2 * ROWS * NODES * FEAT + 2 * NODES * FEAT * FEAT + 2 * ROWS * FEAT * FEAT
 
 
+def make_tokens():
+    toks = [("loadx",)]
+    for c in range(NPASS):
+        toks.append(("load", c, 0))
+    rest = [m for m in range(NCHUNK) if m not in OPEN]
+    for m in rest:
+        toks.append(("load", m, 1))
+    toks.append(("feat",))
+    known = []
+    for c in range(NPASS):
+        toks.append(("rows", c))
+        known.append(c)
+        for m in OPEN:
+            if m == c:
+                toks.append(("prep", m))
+                toks.extend([("pair", m, g, 1) for g in known])
+            elif m in known:
+                toks.append(("pair", m, c, 1))
+    for i, m in enumerate(rest):
+        if i == 0:
+            toks.append(("prep", m))
+        for g in range(NPASS):
+            toks.append(("pair", m, g, 2))
+            if g == PREP_AT and i + 1 < len(rest):
+                toks.append(("prep", rest[i + 1]))
+    toks.append(("drain",))
+    return toks
+
+
 def tile_structureawaregcn_t_kernel(tc, adjacency_matrix, node_features, W_gcn, W_skip, batch_size, out):
     nc = tc.nc
-    x_blocks = node_features.rearrange("(b p) d -> p b d", p=P)
-    out_blocks = out.rearrange("(b p) c -> p b c", p=P)
+    a_groups = adjacency_matrix.rearrange("(G q e) n -> G q e n", q=P, e=2)
+    x_groups = node_features.rearrange("(G q e) d -> q G e d", q=P, e=2)
+    out_groups = out.rearrange("(G q e) c -> G q e c", q=P, e=2)
     with ExitStack() as ctx:
         const = ctx.enter_context(tc.tile_pool(name="const", bufs=1))
         apool = ctx.enter_context(tc.tile_pool(name="apool", bufs=A_SLOTS))
-        stage = ctx.enter_context(tc.tile_pool(name="stage", bufs=6))
-        gpool = ctx.enter_context(tc.tile_pool(name="gpool", bufs=2))
+        ppool = ctx.enter_context(tc.tile_pool(name="ppool", bufs=4))
+        gpool = ctx.enter_context(tc.tile_pool(name="gpool", bufs=4))
         cpool = ctx.enter_context(tc.tile_pool(name="cpool", bufs=3))
+        dpool = ctx.enter_context(tc.tile_pool(name="dpool", bufs=3))
         epool = ctx.enter_context(tc.tile_pool(name="epool", bufs=2))
         psum = ctx.enter_context(tc.psum_pool(name="psum", bufs=4))
+        ctx.enter_context(tc.manual_schedule())
 
         ident_f = const.tile([P, P], F32, name="ident_f")
         ident_b = const.tile([P, P], BF16, name="ident_b")
-        make_identity(nc, ident_f[:])
         make_identity(nc, ident_b[:])
+        make_identity(nc, ident_f[:])
         wT = const.tile([P, 2, 2, FEAT], BF16, name="wT")
         hc = const.tile([P, NPASS, FEAT], U32, name="hc", align_bytes=64)
         hs = const.tile([P, NPASS, FEAT], U8, name="hs", align_bytes=64)
@@ -58,42 +91,41 @@ def tile_structureawaregcn_t_kernel(tc, adjacency_matrix, node_features, W_gcn, 
         nc.vector.memset(warm[:], 1.0)
         nc.scalar.activation(out=warm[:], in_=warm[:], func=ACT.Sqrt)
 
-        a_tiles = {}
+        first = {}
+        second = {}
+        st = {"x": None}
 
-        def load_chunk(c):
-            for blk in range(4 * c, 4 * c + 4):
-                a_t = apool.tile([P, NODES], BF16, name="a_t", tag="a", align_bytes=64)
-                nc.sync.dma_start(out=a_t[:], in_=adjacency_matrix[P * blk : P * blk + P, :])
-                a_tiles[blk] = a_t
+        scratch = apool.tile([P, 2, NODES], BF16, name="scratch", tag="a", align_bytes=64)
+        w_nat = scratch[:, 0, 3072:4096].rearrange("p (w h d) -> p w h d", w=2, h=2)
+        xT_tail = scratch[:, 0, 0:2048].rearrange("p (h n) -> p h n", h=2)
+        nc.sync.dma_start(out=w_nat[:, 0], in_=W_gcn.rearrange("(h p) d -> p h d", p=P))
+        nc.sync.dma_start(out=w_nat[:, 1], in_=W_skip.rearrange("(h p) d -> p h d", p=P))
+
+        def load_x():
+            x_t = apool.tile([P, 2, NODES], BF16, name="x_t", tag="a", align_bytes=64)
+            st["x"] = x_t[:].rearrange("p a n -> p (a n)")
+            nc.sync.dma_start(out=st["x"].rearrange("p (G e d) -> p G e d", e=2, d=FEAT), in_=x_groups)
+
+        def load_chunk(c, again):
+            for G in range(2 * c, 2 * c + 2):
+                a_t = apool.tile([P, 2, NODES], BF16, name="a_t", tag="a", align_bytes=64)
+                nc.sync.dma_start(out=a_t[:], in_=a_groups[G])
+                for e in range(2):
+                    (second if again else first)[2 * G + e] = a_t[:, e, :]
 
         def degrees(c):
             for blk in range(4 * c, 4 * c + 4):
-                a_t = a_tiles[blk]
+                a_b = first[blk]
                 if blk % 2 == 0:
-                    nc.vector.tensor_scalar(out=a_t[:], in0=a_t[:], scalar1=1.0, scalar2=None, op0=ALU.mult, op1=ALU.add, accum_out=deg[:, blk, 0:1])
+                    nc.vector.tensor_scalar(out=a_b, in0=a_b, scalar1=1.0, scalar2=None, op0=ALU.mult, op1=ALU.add, accum_out=deg[:, blk, 0:1])
                 else:
-                    nc.scalar.activation(out=a_t[:], in_=a_t[:], func=ACT.Copy, accum_out=deg[:, blk, 0:1])
+                    nc.scalar.activation(out=a_b, in_=a_b, func=ACT.Copy, accum_out=deg[:, blk, 0:1])
             cols = slice(4 * c, 4 * c + 4)
             nc.scalar.activation(out=sq[:, cols], in_=deg[:, cols, 0], func=ACT.Sqrt, bias=1e-8)
             nc.vector.reciprocal(out=dinv[:, cols], in_=sq[:, cols])
 
-        scratch = apool.tile([P, NODES], BF16, name="scratch", tag="a", align_bytes=64)
-        w_nat = scratch[:, 3072:4096].rearrange("p (w h d) -> p w h d", w=2, h=2)
-        xT_tail = scratch[:, 0:2048].rearrange("p (h n) -> p h n", h=2)
-        gh = scratch[:, 2048:3072].rearrange("p (c t) -> p c t", t=4)
-        nc.sync.dma_start(out=w_nat[:, 0], in_=W_gcn.rearrange("(h p) d -> p h d", p=P))
-        nc.sync.dma_start(out=w_nat[:, 1], in_=W_skip.rearrange("(h p) d -> p h d", p=P))
-        load_chunk(LOAD_ORDER[0])
-        x_nat = []
-        for half in range(2):
-            x_t = apool.tile([P, NODES], BF16, name="x_t", tag="a", align_bytes=64)
-            x_v = x_t[:].rearrange("p (b d) -> p b d", d=FEAT)
-            nc.sync.dma_start(out=x_v, in_=x_blocks[:, 16 * half : 16 * half + 16, :])
-            x_nat.append(x_v)
-        for c in LOAD_ORDER[1:]:
-            load_chunk(c)
-
         def features():
+            x_flat = st["x"]
             wps = psum.tile([P, 2, 2, 2, P], BF16, name="wps", tag="T")
             for w in range(2):
                 for dh in range(2):
@@ -104,11 +136,15 @@ def tile_structureawaregcn_t_kernel(tc, adjacency_matrix, node_features, W_gcn, 
                 for dh in range(2):
                     xps = psum.tile([P, 8, P], BF16, name="xps", tag="T")
                     for nb in range(8):
-                        blk = 8 * q + nb
-                        nc.tensor.transpose(xps[:, nb, :], x_nat[blk // 16][:, blk % 16, P * dh : P * dh + P], ident_b[:])
+                        col = FEAT * (8 * q + nb) + P * dh
+                        nc.tensor.transpose(xps[:, nb, :], x_flat[:, col : col + P], ident_b[:])
                     dst = xT[:, dh, 1024 * q : 1024 * q + 1024] if q < 3 else xT_tail[:, dh, :]
-                    nc.scalar.copy(out=dst, in_=xps[:].rearrange("p b n -> p (b n)"))
+                    if dh == 0:
+                        nc.scalar.copy(out=dst, in_=xps[:].rearrange("p b n -> p (b n)"))
+                    else:
+                        nc.vector.tensor_copy(out=dst, in_=xps[:].rearrange("p b n -> p (b n)"))
             for g in range(NPASS):
+                gh = x_flat[:, 1024 * g : 1024 * g + 1024].rearrange("p (c t) -> p c t", t=4)
                 for ch in range(2):
                     hps = psum.tile([P, 4, P], F32, name="hps", tag="T")
                     for t in range(4):
@@ -116,49 +152,26 @@ def tile_structureawaregcn_t_kernel(tc, adjacency_matrix, node_features, W_gcn, 
                         for dh in range(2):
                             lhsT = xT[:, dh, P * blk : P * blk + P] if blk < MBLK else xT_tail[:, dh, P * (blk - MBLK) : P * (blk - MBLK) + P]
                             nc.tensor.matmul(out=hps[:, t, :], lhsT=lhsT, rhs=wT[:, 0, dh, P * ch : P * ch + P], start=(dh == 0), stop=(dh == 1))
-                    nc.scalar.copy(out=gh[:, P * ch : P * ch + P, :], in_=hps[:].rearrange("p t c -> p c t"))
-                nc.vector.quantize_mx(out=hc[:, g, :].bitcast(FP8X4), scales=hs[:, g, :], in_=gh.rearrange("p c t -> p (c t)"))
+                    nc.vector.tensor_copy(out=gh[:, P * ch : P * ch + P, :], in_=hps[:].rearrange("p t c -> p c t"))
+                nc.vector.quantize_mx(out=hc[:, g, :].bitcast(FP8X4), scales=hs[:, g, :], in_=x_flat[:, 1024 * g : 1024 * g + 1024])
 
-        counter = [0]
-        pending = []
+        toks = make_tokens()
+        pairs = [t for t in toks if t[0] == "pair"]
+        work = [{} for t in pairs]
         acc = {}
         seen = {}
+        drow = {}
+        wsm = {}
+        fin = []
 
-        def flush_pending():
-            while pending:
-                m, g, grp = pending.pop(0)
-                codes = cpool.tile([P, PASS], U32, name="codes", align_bytes=64)
-                scl = cpool.tile([P, PASS], U8, name="scl", align_bytes=64)
-                nc.vector.quantize_mx(out=codes[:].bitcast(FP8X4), scales=scl[:], in_=grp[:].rearrange("p r t -> p (r t)"))
-                seen[m] = seen.get(m, 0) + 1
-                for ch in range(2):
-                    nc.tensor.matmul_mx(out=acc[m][ch][:], lhsT=hc[:, g, P * ch : P * ch + P].bitcast(FP8X4), lhsT_scale=hs[:, g, P * ch : P * ch + P], rhs=codes[:].bitcast(FP8X4), rhs_scale=scl[:], start=(seen[m] == 1), stop=(seen[m] == NPASS))
-
-        def pair(m, g, pattern):
-            if m not in acc:
-                acc[m] = [psum.tile([P, PASS], F32, name="acc", tag="acc") for ch in range(2)]
-            grp = gpool.tile([P, PASS, 4], BF16, name="grp", align_bytes=64)
+        def prep(m):
+            dps = psum.tile([P, 4, P], F32, name="dps", tag="T")
             for j in range(4):
                 b = 4 * m + j
-                src = a_tiles[b][:, PASS * g : PASS * g + PASS]
-                f = stage.tile([P, PASS], F32, name="f")
-                eng = pattern[counter[0] % len(pattern)]
-                counter[0] += 1
-                if eng == "g":
-                    nc.gpsimd.tensor_scalar(out=f[:], in0=src, scalar1=dinv[:, b : b + 1], scalar2=0.0, op0=ALU.mult, op1=ALU.add)
-                elif eng == "s":
-                    nc.scalar.activation(out=f[:], in_=src, func=ACT.Copy, scale=dinv[:, b : b + 1])
-                else:
-                    nc.vector.tensor_scalar(out=f[:], in0=src, scalar1=dinv[:, b : b + 1], scalar2=None, op0=ALU.mult)
-                bank = psum.tile([P, 4, P], F32, name="bank", tag="T")
-                for t in range(4):
-                    nc.tensor.transpose(bank[:, t, :], f[:, P * t : P * t + P], ident_f[:])
-                nc.vector.tensor_tensor(out=grp[:, P * j : P * j + P, :], in0=bank[:].rearrange("p t r -> p r t"), in1=dinv[:, 4 * g : 4 * g + 4].unsqueeze(1).to_broadcast([P, P, 4]), op=ALU.mult)
-                if j == 0:
-                    flush_pending()
-            pending.append((m, g, grp))
-
-        def skip_term(m):
+                nc.tensor.transpose(dps[:, j, :], dinv[:, b : b + 1].to_broadcast([P, P]), ident_f[:])
+            dr = dpool.tile([P, PASS], F32, name="dr")
+            nc.scalar.copy(out=dr[:], in_=dps[:].rearrange("p j r -> p (j r)"))
+            drow[m] = dr
             ws = []
             for ch in range(2):
                 skp = psum.tile([P, PASS], F32, name="skp", tag="T")
@@ -167,46 +180,99 @@ def tile_structureawaregcn_t_kernel(tc, adjacency_matrix, node_features, W_gcn, 
                 w = epool.tile([P, PASS], F32, name="w%d" % ch)
                 nc.scalar.activation(out=w[:], in_=skp[:], func=ACT.Copy, scale=0.5)
                 ws.append(w)
-            return ws
+            wsm[m] = ws
 
-        def finish(m, ws):
+        def stage_t(k):
+            if k >= len(pairs):
+                return
+            m, g, ph = pairs[k][1], pairs[k][2], pairs[k][3]
+            src = second if ph == 2 else first
+            banks = []
+            for u in range(2):
+                bank = psum.tile([P, 4, P], F32, name="bank", tag="T")
+                col = 256 * g + P * u
+                for j in range(4):
+                    nc.tensor.transpose(bank[:, j, :], src[4 * m + j].bitcast(F32)[:, col : col + P], ident_f[:])
+                banks.append(bank)
+            work[k]["banks"] = banks
+
+        def stage_v(k):
+            m, g = pairs[k][1], pairs[k][2]
+            planes = ppool.tile([P, 4, PASS], BF16, name="planes")
+            for u in range(2):
+                halves = work[k]["banks"][u][:].rearrange("p j r -> p (j r)").bitcast(BF16).rearrange("p (x e) -> p x e", e=2)
+                for e in range(2):
+                    t = 2 * u + e
+                    nc.vector.scalar_tensor_tensor(out=planes[:, t, :], in0=halves[:, :, e], scalar=dinv[:, 4 * g + t : 4 * g + t + 1], in1=drow[m][:], op0=ALU.mult, op1=ALU.mult)
+            work[k]["planes"] = planes
+
+        def stage_r(k):
+            planes = work[k]["planes"]
+            grp = gpool.tile([P, PASS, 4], BF16, name="grp", align_bytes=64)
+            if pairs[k][3] == 1:
+                nc.gpsimd.tensor_scalar(out=grp[:], in0=planes[:].rearrange("p t x -> p x t"), scalar1=1.0, scalar2=0.0, op0=ALU.mult, op1=ALU.add)
+            else:
+                nc.scalar.copy(out=grp[:].rearrange("p (c i) t -> p c t i", i=4), in_=planes[:].rearrange("p t (c i) -> p c t i", i=4))
+            work[k]["grp"] = grp
+
+        def stage_q(k):
+            m, g = pairs[k][1], pairs[k][2]
+            if m not in acc:
+                acc[m] = [psum.tile([P, PASS], F32, name="acc", tag="acc") for ch in range(2)]
+            codes = cpool.tile([P, PASS], U32, name="codes", align_bytes=64)
+            scl = cpool.tile([P, PASS], U8, name="scl", align_bytes=64)
+            nc.vector.quantize_mx(out=codes[:].bitcast(FP8X4), scales=scl[:], in_=work[k]["grp"][:].rearrange("p x t -> p (x t)"))
+            seen[m] = seen.get(m, 0) + 1
+            for ch in range(2):
+                nc.tensor.matmul_mx(out=acc[m][ch][:], lhsT=hc[:, g, P * ch : P * ch + P].bitcast(FP8X4), lhsT_scale=hs[:, g, P * ch : P * ch + P], rhs=codes[:].bitcast(FP8X4), rhs_scale=scl[:], start=(seen[m] == 1), stop=(seen[m] == NPASS))
+            if seen[m] == NPASS:
+                fin.append((m, k + FIN_DELAY))
+
+        def finish(m):
+            ws = wsm[m]
             for ch in range(2):
                 w = ws[ch]
                 nc.vector.scalar_tensor_tensor(out=w[:], in0=acc[m][ch][:], scalar=0.5, in1=w[:], op0=ALU.mult, op1=ALU.add)
                 nc.vector.scalar_tensor_tensor(out=w[:], in0=w[:], scalar=0.0, in1=xT[:, ch, PASS * m : PASS * m + PASS], op0=ALU.max, op1=ALU.add)
             for jp in range(2):
                 bo = psum.tile([P, 2, 2, P], F32, name="bo", tag="T")
-                for j in range(2):
+                for e in range(2):
                     for ch in range(2):
-                        col = P * (2 * jp + j)
-                        nc.tensor.transpose(bo[:, j, ch, :], ws[ch][:, col : col + P], ident_f[:])
+                        col = P * (2 * jp + e)
+                        nc.tensor.transpose(bo[:, e, ch, :], ws[ch][:, col : col + P], ident_f[:])
                 o = epool.tile([P, 2, FEAT], F32, name="o")
-                nc.scalar.copy(out=o[:].rearrange("p j c -> p (j c)"), in_=bo[:].rearrange("p j h c -> p (j h c)"))
-                nc.sync.dma_start(out=out_blocks[:, 4 * m + 2 * jp : 4 * m + 2 * jp + 2, :], in_=o[:])
+                nc.scalar.copy(out=o[:].rearrange("p e c -> p (e c)"), in_=bo[:].rearrange("p e h c -> p (e h c)"))
+                nc.scalar.dma_start(out=out_groups[2 * m + jp], in_=o[:])
 
-        known = []
-        ws_open = {}
-        for step, c in enumerate(LOAD_ORDER):
-            degrees(c)
-            if step == 0:
+        k = 0
+        qd = 0
+        for tok in toks:
+            kind = tok[0]
+            if kind == "loadx":
+                load_x()
+            elif kind == "load":
+                load_chunk(tok[1], tok[2])
+            elif kind == "feat":
                 features()
-            known.append(c)
-            for m in OPEN:
-                if m == c:
-                    ws_open[m] = skip_term(m)
-                    for g in known:
-                        pair(m, g, NAT1)
-                elif m in known:
-                    pair(m, c, NAT1)
-        flush_pending()
-        for m in OPEN:
-            finish(m, ws_open[m])
-        for m in range(ROWS // PASS):
-            if m in OPEN:
-                continue
-            load_chunk(m)
-            ws = skip_term(m)
-            for g in range(NPASS):
-                pair(m, g, NAT2)
-            flush_pending()
-            finish(m, ws)
+            elif kind == "rows":
+                degrees(tok[1])
+            elif kind == "prep":
+                prep(tok[1])
+            elif kind == "pair":
+                if k == 0:
+                    stage_t(0)
+                stage_t(k + 1)
+                stage_v(k)
+                stage_r(k)
+                if k - LAG >= qd:
+                    stage_q(qd)
+                    qd += 1
+                k += 1
+                while fin and fin[0][1] <= k:
+                    finish(fin.pop(0)[0])
+            else:
+                while qd < k:
+                    stage_q(qd)
+                    qd += 1
+                while fin:
+                    finish(fin.pop(0)[0])

from contextlib import ExitStack

import concourse.bass as bass
import concourse.mybir as mybir
import concourse.tile as tile
from concourse.masks import make_identity

F32 = mybir.dt.float32
BF16 = mybir.dt.bfloat16
U8 = mybir.dt.uint8
U32 = mybir.dt.uint32
FP8X4 = mybir.dt.float8_e4m3fn_x4
ALU = mybir.AluOpType
ACT = mybir.ActivationFunctionType

P = 128
NODES = 4096
FEAT = 256
ROWS = 3072
NBLK = NODES // P
MBLK = ROWS // P
PASS = 512
NPASS = NODES // PASS
NCHUNK = ROWS // PASS
OPEN = [0, 1]
A_SLOTS = 9
LAG = 2
FIN_DELAY = 2
PREP_AT = 3

FLOPS = 2 * ROWS * NODES * FEAT + 2 * NODES * FEAT * FEAT + 2 * ROWS * FEAT * FEAT


def make_tokens():
    toks = [("loadx",)]
    for c in range(NPASS):
        toks.append(("load", c, 0))
    rest = [m for m in range(NCHUNK) if m not in OPEN]
    for m in rest:
        toks.append(("load", m, 1))
    toks.append(("feat",))
    known = []
    for c in range(NPASS):
        toks.append(("rows", c))
        known.append(c)
        for m in OPEN:
            if m == c:
                toks.append(("prep", m))
                toks.extend([("pair", m, g, 1) for g in known])
            elif m in known:
                toks.append(("pair", m, c, 1))
    for i, m in enumerate(rest):
        if i == 0:
            toks.append(("prep", m))
        for g in range(NPASS):
            toks.append(("pair", m, g, 2))
            if g == PREP_AT and i + 1 < len(rest):
                toks.append(("prep", rest[i + 1]))
    toks.append(("drain",))
    return toks


def tile_structureawaregcn_t_kernel(tc, adjacency_matrix, node_features, W_gcn, W_skip, batch_size, out):
    nc = tc.nc
    a_groups = adjacency_matrix.rearrange("(G q e) n -> G q e n", q=P, e=2)
    x_groups = node_features.rearrange("(G q e) d -> q G e d", q=P, e=2)
    out_groups = out.rearrange("(G q e) c -> G q e c", q=P, e=2)
    with ExitStack() as ctx:
        const = ctx.enter_context(tc.tile_pool(name="const", bufs=1))
        apool = ctx.enter_context(tc.tile_pool(name="apool", bufs=A_SLOTS))
        ppool = ctx.enter_context(tc.tile_pool(name="ppool", bufs=4))
        gpool = ctx.enter_context(tc.tile_pool(name="gpool", bufs=4))
        cpool = ctx.enter_context(tc.tile_pool(name="cpool", bufs=3))
        dpool = ctx.enter_context(tc.tile_pool(name="dpool", bufs=3))
        epool = ctx.enter_context(tc.tile_pool(name="epool", bufs=2))
        psum = ctx.enter_context(tc.psum_pool(name="psum", bufs=4))
        ctx.enter_context(tc.manual_schedule())

        ident_f = const.tile([P, P], F32, name="ident_f")
        ident_b = const.tile([P, P], BF16, name="ident_b")
        make_identity(nc, ident_b[:])
        make_identity(nc, ident_f[:])
        wT = const.tile([P, 2, 2, FEAT], BF16, name="wT")
        hc = const.tile([P, NPASS, FEAT], U32, name="hc", align_bytes=64)
        hs = const.tile([P, NPASS, FEAT], U8, name="hs", align_bytes=64)
        xT = const.tile([P, 2, ROWS], BF16, name="xT")
        deg = const.tile([P, NBLK, 8], F32, name="deg")
        sq = const.tile([P, NBLK], F32, name="sq")
        dinv = const.tile([P, NBLK], F32, name="dinv")
        warm = const.tile([P, 1], F32, name="warm")
        nc.vector.memset(warm[:], 1.0)
        nc.scalar.activation(out=warm[:], in_=warm[:], func=ACT.Sqrt)

        first = {}
        second = {}
        st = {"x": None}

        scratch = apool.tile([P, 2, NODES], BF16, name="scratch", tag="a", align_bytes=64)
        w_nat = scratch[:, 0, 3072:4096].rearrange("p (w h d) -> p w h d", w=2, h=2)
        xT_tail = scratch[:, 0, 0:2048].rearrange("p (h n) -> p h n", h=2)
        nc.sync.dma_start(out=w_nat[:, 0], in_=W_gcn.rearrange("(h p) d -> p h d", p=P))
        nc.sync.dma_start(out=w_nat[:, 1], in_=W_skip.rearrange("(h p) d -> p h d", p=P))

        def load_x():
            x_t = apool.tile([P, 2, NODES], BF16, name="x_t", tag="a", align_bytes=64)
            st["x"] = x_t[:].rearrange("p a n -> p (a n)")
            nc.sync.dma_start(out=st["x"].rearrange("p (G e d) -> p G e d", e=2, d=FEAT), in_=x_groups)

        def load_chunk(c, again):
            for G in range(2 * c, 2 * c + 2):
                a_t = apool.tile([P, 2, NODES], BF16, name="a_t", tag="a", align_bytes=64)
                nc.sync.dma_start(out=a_t[:], in_=a_groups[G])
                for e in range(2):
                    (second if again else first)[2 * G + e] = a_t[:, e, :]

        def degrees(c):
            for blk in range(4 * c, 4 * c + 4):
                a_b = first[blk]
                if blk % 2 == 0:
                    nc.vector.tensor_scalar(out=a_b, in0=a_b, scalar1=1.0, scalar2=None, op0=ALU.mult, op1=ALU.add, accum_out=deg[:, blk, 0:1])
                else:
                    nc.scalar.activation(out=a_b, in_=a_b, func=ACT.Copy, accum_out=deg[:, blk, 0:1])
            cols = slice(4 * c, 4 * c + 4)
            nc.scalar.activation(out=sq[:, cols], in_=deg[:, cols, 0], func=ACT.Sqrt, bias=1e-8)
            nc.vector.reciprocal(out=dinv[:, cols], in_=sq[:, cols])

        def features():
            x_flat = st["x"]
            wps = psum.tile([P, 2, 2, 2, P], BF16, name="wps", tag="T")
            for w in range(2):
                for dh in range(2):
                    for oh in range(2):
                        nc.tensor.transpose(wps[:, w, dh, oh, :], w_nat[:, w, oh, P * dh : P * dh + P], ident_b[:])
            nc.scalar.copy(out=wT[:].rearrange("p w h o -> p (w h o)"), in_=wps[:].rearrange("p w h q o -> p (w h q o)"))
            for q in range(4):
                for dh in range(2):
                    xps = psum.tile([P, 8, P], BF16, name="xps", tag="T")
                    for nb in range(8):
                        col = FEAT * (8 * q + nb) + P * dh
                        nc.tensor.transpose(xps[:, nb, :], x_flat[:, col : col + P], ident_b[:])
                    dst = xT[:, dh, 1024 * q : 1024 * q + 1024] if q < 3 else xT_tail[:, dh, :]
                    if dh == 0:
                        nc.scalar.copy(out=dst, in_=xps[:].rearrange("p b n -> p (b n)"))
                    else:
                        nc.vector.tensor_copy(out=dst, in_=xps[:].rearrange("p b n -> p (b n)"))
            for g in range(NPASS):
                gh = x_flat[:, 1024 * g : 1024 * g + 1024].rearrange("p (c t) -> p c t", t=4)
                for ch in range(2):
                    hps = psum.tile([P, 4, P], F32, name="hps", tag="T")
                    for t in range(4):
                        blk = 4 * g + t
                        for dh in range(2):
                            lhsT = xT[:, dh, P * blk : P * blk + P] if blk < MBLK else xT_tail[:, dh, P * (blk - MBLK) : P * (blk - MBLK) + P]
                            nc.tensor.matmul(out=hps[:, t, :], lhsT=lhsT, rhs=wT[:, 0, dh, P * ch : P * ch + P], start=(dh == 0), stop=(dh == 1))
                    nc.vector.tensor_copy(out=gh[:, P * ch : P * ch + P, :], in_=hps[:].rearrange("p t c -> p c t"))
                nc.vector.quantize_mx(out=hc[:, g, :].bitcast(FP8X4), scales=hs[:, g, :], in_=x_flat[:, 1024 * g : 1024 * g + 1024])

        toks = make_tokens()
        pairs = [t for t in toks if t[0] == "pair"]
        work = [{} for t in pairs]
        acc = {}
        seen = {}
        drow = {}
        wsm = {}
        fin = []

        def prep(m):
            dps = psum.tile([P, 4, P], F32, name="dps", tag="T")
            for j in range(4):
                b = 4 * m + j
                nc.tensor.transpose(dps[:, j, :], dinv[:, b : b + 1].to_broadcast([P, P]), ident_f[:])
            dr = dpool.tile([P, PASS], F32, name="dr")
            nc.scalar.copy(out=dr[:], in_=dps[:].rearrange("p j r -> p (j r)"))
            drow[m] = dr
            ws = []
            for ch in range(2):
                skp = psum.tile([P, PASS], F32, name="skp", tag="T")
                for dh in range(2):
                    nc.tensor.matmul(out=skp[:], lhsT=wT[:, 1, dh, P * ch : P * ch + P], rhs=xT[:, dh, PASS * m : PASS * m + PASS], start=(dh == 0), stop=(dh == 1))
                w = epool.tile([P, PASS], F32, name="w%d" % ch)
                nc.scalar.activation(out=w[:], in_=skp[:], func=ACT.Copy, scale=0.5)
                ws.append(w)
            wsm[m] = ws

        def stage_t(k):
            if k >= len(pairs):
                return
            m, g, ph = pairs[k][1], pairs[k][2], pairs[k][3]
            src = second if ph == 2 else first
            banks = []
            for u in range(2):
                bank = psum.tile([P, 4, P], F32, name="bank", tag="T")
                col = 256 * g + P * u
                for j in range(4):
                    nc.tensor.transpose(bank[:, j, :], src[4 * m + j].bitcast(F32)[:, col : col + P], ident_f[:])
                banks.append(bank)
            work[k]["banks"] = banks

        def stage_v(k):
            m, g = pairs[k][1], pairs[k][2]
            planes = ppool.tile([P, 4, PASS], BF16, name="planes")
            for u in range(2):
                halves = work[k]["banks"][u][:].rearrange("p j r -> p (j r)").bitcast(BF16).rearrange("p (x e) -> p x e", e=2)
                for e in range(2):
                    t = 2 * u + e
                    nc.vector.scalar_tensor_tensor(out=planes[:, t, :], in0=halves[:, :, e], scalar=dinv[:, 4 * g + t : 4 * g + t + 1], in1=drow[m][:], op0=ALU.mult, op1=ALU.mult)
            work[k]["planes"] = planes

        def stage_r(k):
            planes = work[k]["planes"]
            grp = gpool.tile([P, PASS, 4], BF16, name="grp", align_bytes=64)
            if pairs[k][3] == 1:
                nc.gpsimd.tensor_scalar(out=grp[:], in0=planes[:].rearrange("p t x -> p x t"), scalar1=1.0, scalar2=0.0, op0=ALU.mult, op1=ALU.add)
            else:
                nc.scalar.copy(out=grp[:].rearrange("p (c i) t -> p c t i", i=4), in_=planes[:].rearrange("p t (c i) -> p c t i", i=4))
            work[k]["grp"] = grp

        def stage_q(k):
            m, g = pairs[k][1], pairs[k][2]
            if m not in acc:
                acc[m] = [psum.tile([P, PASS], F32, name="acc", tag="acc") for ch in range(2)]
            codes = cpool.tile([P, PASS], U32, name="codes", align_bytes=64)
            scl = cpool.tile([P, PASS], U8, name="scl", align_bytes=64)
            nc.vector.quantize_mx(out=codes[:].bitcast(FP8X4), scales=scl[:], in_=work[k]["grp"][:].rearrange("p x t -> p (x t)"))
            seen[m] = seen.get(m, 0) + 1
            for ch in range(2):
                nc.tensor.matmul_mx(out=acc[m][ch][:], lhsT=hc[:, g, P * ch : P * ch + P].bitcast(FP8X4), lhsT_scale=hs[:, g, P * ch : P * ch + P], rhs=codes[:].bitcast(FP8X4), rhs_scale=scl[:], start=(seen[m] == 1), stop=(seen[m] == NPASS))
            if seen[m] == NPASS:
                fin.append((m, k + FIN_DELAY))

        def finish(m):
            ws = wsm[m]
            for ch in range(2):
                w = ws[ch]
                nc.vector.scalar_tensor_tensor(out=w[:], in0=acc[m][ch][:], scalar=0.5, in1=w[:], op0=ALU.mult, op1=ALU.add)
                nc.vector.scalar_tensor_tensor(out=w[:], in0=w[:], scalar=0.0, in1=xT[:, ch, PASS * m : PASS * m + PASS], op0=ALU.max, op1=ALU.add)
            for jp in range(2):
                bo = psum.tile([P, 2, 2, P], F32, name="bo", tag="T")
                for e in range(2):
                    for ch in range(2):
                        col = P * (2 * jp + e)
                        nc.tensor.transpose(bo[:, e, ch, :], ws[ch][:, col : col + P], ident_f[:])
                o = epool.tile([P, 2, FEAT], F32, name="o")
                nc.scalar.copy(out=o[:].rearrange("p e c -> p (e c)"), in_=bo[:].rearrange("p e h c -> p (e h c)"))
                nc.scalar.dma_start(out=out_groups[2 * m + jp], in_=o[:])

        k = 0
        qd = 0
        for tok in toks:
            kind = tok[0]
            if kind == "loadx":
                load_x()
            elif kind == "load":
                load_chunk(tok[1], tok[2])
            elif kind == "feat":
                features()
            elif kind == "rows":
                degrees(tok[1])
            elif kind == "prep":
                prep(tok[1])
            elif kind == "pair":
                if k == 0:
                    stage_t(0)
                stage_t(k + 1)
                stage_v(k)
                stage_r(k)
                if k - LAG >= qd:
                    stage_q(qd)
                    qd += 1
                k += 1
                while fin and fin[0][1] <= k:
                    finish(fin.pop(0)[0])
            else:
                while qd < k:
                    stage_q(qd)
                    qd += 1
                while fin:
                    finish(fin.pop(0)[0])
